import numpy as np
import ml_dtypes

BF16 = ml_dtypes.bfloat16


def bf(x):
    return np.asarray(x, np.float32).astype(BF16)


def f32(x):
    return np.asarray(x, np.float32)


def f64(x):
    return np.asarray(x).astype(np.float64)


def striped(idx):
    return np.tile(idx.reshape(-1, 16).T, (8, 1))


V, D, H, M, P, N = 512, 128, 128, 512, 256, 768


def sigmoid(v):
    return 1.0 / (1.0 + np.exp(-v))


def setup_inputs():
    return {
        "table": bf(np.random.standard_normal((D, V))),
        "w": bf(np.random.standard_normal((D, M)) / np.sqrt(D)),
        "r": bf(3.0 * np.random.standard_normal((H, M)) / np.sqrt(H)),
        "b": f32(0.3 * np.random.standard_normal((M, 1))),
        "offs": striped(np.random.permutation(np.tile(np.arange(V), 2))[:N]),
    }


def reference(table, w, r, b, offs):
    idx = offs[:16].T.reshape(-1)
    z = f64(w).T @ f64(table)[:, idx] + f64(b)
    zi, zo, zu, zf = z.reshape(-1, H, N)
    ri, ro, ru, rf = f64(r).T.reshape(-1, H, H)
    c_leaf = sigmoid(zi[:, P:]) * np.tanh(zu[:, P:])
    h_leaf = sigmoid(zo[:, P:]) * np.tanh(c_leaf)
    hs = h_leaf[:, 0::2] + h_leaf[:, 1::2]
    f = sigmoid(np.repeat(zf[:, :P], 2, axis=1) + rf @ h_leaf)
    fc = f * c_leaf
    c_par = sigmoid(zi[:, :P] + ri @ hs) * np.tanh(zu[:, :P] + ru @ hs) + fc[:, 0::2] + fc[:, 1::2]
    h_par = sigmoid(zo[:, :P] + ro @ hs) * np.tanh(c_par)
    return np.concatenate([h_par, h_leaf], axis=1)

@@ -1,0 +1,124 @@
+import concourse.mybir as mybir
+
+BF16, F32, U16 = mybir.dt.bfloat16, mybir.dt.float32, mybir.dt.uint16
+SIGMOID = mybir.ActivationFunctionType.Sigmoid
+TANH = mybir.ActivationFunctionType.Tanh
+MULT, ADD = mybir.AluOpType.mult, mybir.AluOpType.add
+
+H = 128
+V = 512
+N = 768
+PARENTS = 256
+GATE_I, GATE_O, GATE_U, GATE_F = 0, 1, 2, 3
+
+CHUNKS = 1
+PC = PARENTS // CHUNKS
+LC = 2 * PC
+
+FLOPS = 2 * H * H * (3 * 2 * PARENTS + 4 * PARENTS + 3 * PARENTS + 2 * PARENTS)
+
+
+def tile_treemodel_kernel(tc, table, w, r, b, offs, out):
+    nc = tc.nc
+    with (
+        tc.tile_pool(name="held", bufs=1) as held,
+        tc.tile_pool(name="work", bufs=CHUNKS) as work,
+        tc.psum_pool(name="psum", bufs=8) as psum,
+    ):
+        offsets = held.tile([H, N // 16], U16, name="offsets")
+        nc.sync.dma_start(offsets[:], offs)
+        table_sb = held.tile([H, V], BF16, name="table_sb")
+        nc.sync.dma_start(table_sb[:], table)
+        w_sb = held.tile([H, 4 * H], BF16, name="w_sb")
+        nc.scalar.dma_start(w_sb[:], w)
+        bias = held.tile([H, 4], F32, name="bias")
+        with nc.allow_non_contiguous_dma(reason="512 floats, one to a partition and gate"):
+            nc.scalar.dma_start(bias[:], b.rearrange("(g n) one -> n (g one)", n=H))
+        r_sb = held.tile([H, 4 * H], BF16, name="r_sb")
+        nc.sync.dma_start(r_sb[:], r)
+
+        def block(weights, gate):
+            return weights[:, gate * H : (gate + 1) * H]
+
+        def looked_up(first, count):
+            return table_sb[:].indirect(offsets[:, first // 16 : (first + count) // 16])
+
+        def activate(name, width, func, source, gate):
+            result = work.tile([H, width], F32, name=name)
+            nc.scalar.activation(result[:], source, func, bias=bias[:, gate : gate + 1])
+            return result
+
+        def split(tile_ap):
+            return tile_ap.rearrange("p (j two) -> p two j", two=2)
+
+        def halves(tile_ap):
+            return tile_ap.rearrange("p (two j) -> p two j", two=2)
+
+        z_leaf, z_parent = [], []
+        for k in range(CHUNKS):
+            z = {}
+            for gate in (GATE_I, GATE_U, GATE_O):
+                z[gate] = psum.tile([H, LC], F32, name=f"z_leaf{gate}", tag="bank")
+                nc.tensor.matmul(
+                    z[gate][:], block(w_sb, gate), looked_up(PARENTS + k * LC, LC), start=True, stop=True
+                )
+            z_leaf.append(z)
+        for k in range(CHUNKS):
+            z = {}
+            for gate in (GATE_I, GATE_U, GATE_O):
+                z[gate] = psum.tile([H, PC], F32, name=f"z_parent{gate}", tag="bank")
+                nc.tensor.matmul(z[gate][:], block(w_sb, gate), looked_up(k * PC, PC), start=True, stop=False)
+            z[GATE_F] = psum.tile([H, LC], F32, name="z_forget", tag="bank")
+            for child in range(2):
+                nc.tensor.matmul(
+                    z[GATE_F][:, child * PC : (child + 1) * PC],
+                    block(w_sb, GATE_F),
+                    looked_up(k * PC, PC),
+                    start=(child == 0),
+                    stop=False,
+                )
+            z_parent.append(z)
+
+        c_leaves, h_children, h_sums = [], [], []
+        for k in range(CHUNKS):
+            z = z_leaf[k]
+            i_leaf = activate("i_leaf", LC, SIGMOID, z[GATE_I][:], GATE_I)
+            u_leaf = activate("u_leaf", LC, TANH, z[GATE_U][:], GATE_U)
+            c_leaf = work.tile([H, LC], F32, name="c_leaf")
+            nc.vector.tensor_tensor(c_leaf[:], i_leaf[:], u_leaf[:], MULT)
+            o_leaf = activate("o_leaf", LC, SIGMOID, z[GATE_O][:], GATE_O)
+            tanh_c_leaf = work.tile([H, LC], F32, name="tanh_c_leaf")
+            nc.scalar.activation(tanh_c_leaf[:], c_leaf[:], TANH)
+            h_leaf = work.tile([H, LC], F32, name="h_leaf")
+            nc.vector.tensor_tensor(h_leaf[:], o_leaf[:], tanh_c_leaf[:], MULT)
+            nc.sync.dma_start(out[:, PARENTS + k * LC : PARENTS + (k + 1) * LC], h_leaf[:])
+            h_child = work.tile([H, LC], BF16, name="h_child")
+            nc.vector.tensor_copy(halves(h_child[:]), split(h_leaf[:]))
+            h_sum = work.tile([H, PC], BF16, name="h_sum")
+            nc.vector.tensor_tensor(h_sum[:], split(h_leaf[:])[:, 0, :], split(h_leaf[:])[:, 1, :], ADD)
+            c_leaves.append(c_leaf)
+            h_children.append(h_child)
+            h_sums.append(h_sum)
+
+        for k in range(CHUNKS):
+            z = z_parent[k]
+            nc.tensor.matmul(z[GATE_F][:], block(r_sb, GATE_F), h_children[k][:], start=False, stop=True)
+            for gate in (GATE_I, GATE_U, GATE_O):
+                nc.tensor.matmul(z[gate][:], block(r_sb, gate), h_sums[k][:], start=False, stop=True)
+            f_child = activate("f_child", LC, SIGMOID, z[GATE_F][:], GATE_F)
+            fc_child = work.tile([H, LC], F32, name="fc_child")
+            nc.vector.tensor_tensor(halves(fc_child[:]), halves(f_child[:]), split(c_leaves[k][:]), MULT)
+            i_parent = activate("i_parent", PC, SIGMOID, z[GATE_I][:], GATE_I)
+            u_parent = activate("u_parent", PC, TANH, z[GATE_U][:], GATE_U)
+            o_parent = activate("o_parent", PC, SIGMOID, z[GATE_O][:], GATE_O)
+            fc_sum = work.tile([H, PC], F32, name="fc_sum")
+            nc.vector.tensor_tensor(fc_sum[:], fc_child[:, :PC], fc_child[:, PC:], ADD)
+            iu_parent = work.tile([H, PC], F32, name="iu_parent")
+            nc.vector.tensor_tensor(iu_parent[:], i_parent[:], u_parent[:], MULT)
+            c_parent = work.tile([H, PC], F32, name="c_parent")
+            nc.vector.tensor_tensor(c_parent[:], iu_parent[:], fc_sum[:], ADD)
+            tanh_c_parent = work.tile([H, PC], F32, name="tanh_c_parent")
+            nc.scalar.activation(tanh_c_parent[:], c_parent[:], TANH)
+            h_parent = work.tile([H, PC], F32, name="h_parent")
+            nc.vector.tensor_tensor(h_parent[:], o_parent[:], tanh_c_parent[:], MULT)
+            nc.sync.dma_start(out[:, k * PC : (k + 1) * PC], h_parent[:])

@@ -28,14 +28,18 @@ def tile_treemodel_kernel(tc, table, w, r, b, offs, out):
         offsets = held.tile([H, N // 16], U16, name="offsets")
         nc.sync.dma_start(offsets[:], offs)
         table_sb = held.tile([H, V], BF16, name="table_sb")
-        nc.sync.dma_start(table_sb[:], table)
+        nc.scalar.dma_start(table_sb[:], table)
         w_sb = held.tile([H, 4 * H], BF16, name="w_sb")
-        nc.scalar.dma_start(w_sb[:], w)
+        nc.sync.dma_start(w_sb[:], w)
         bias = held.tile([H, 4], F32, name="bias")
         with nc.allow_non_contiguous_dma(reason="512 floats, one to a partition and gate"):
             nc.scalar.dma_start(bias[:], b.rearrange("(g n) one -> n (g one)", n=H))
         r_sb = held.tile([H, 4 * H], BF16, name="r_sb")
         nc.sync.dma_start(r_sb[:], r)
+
+        warm = held.tile([H, 1], F32, name="warm")
+        nc.vector.memset(warm[:], 0.0)
+        nc.scalar.activation(warm[:], warm[:], SIGMOID)
 
         def block(weights, gate):
             return weights[:, gate * H : (gate + 1) * H]

@@ -11,7 +11,7 @@ N = 768
 PARENTS = 256
 GATE_I, GATE_O, GATE_U, GATE_F = 0, 1, 2, 3
 
-CHUNKS = 1
+CHUNKS = 2
 PC = PARENTS // CHUNKS
 LC = 2 * PC
 
@@ -83,46 +83,49 @@ def tile_treemodel_kernel(tc, table, w, r, b, offs, out):
                 )
             z_parent.append(z)
 
-        c_leaves, h_children, h_sums = [], [], []
+        c_leaf, o_leaf = [], []
         for k in range(CHUNKS):
             z = z_leaf[k]
             i_leaf = activate("i_leaf", LC, SIGMOID, z[GATE_I][:], GATE_I)
             u_leaf = activate("u_leaf", LC, TANH, z[GATE_U][:], GATE_U)
-            c_leaf = work.tile([H, LC], F32, name="c_leaf")
-            nc.vector.tensor_tensor(c_leaf[:], i_leaf[:], u_leaf[:], MULT)
-            o_leaf = activate("o_leaf", LC, SIGMOID, z[GATE_O][:], GATE_O)
-            tanh_c_leaf = work.tile([H, LC], F32, name="tanh_c_leaf")
-            nc.scalar.activation(tanh_c_leaf[:], c_leaf[:], TANH)
-            h_leaf = work.tile([H, LC], F32, name="h_leaf")
-            nc.vector.tensor_tensor(h_leaf[:], o_leaf[:], tanh_c_leaf[:], MULT)
-            nc.sync.dma_start(out[:, PARENTS + k * LC : PARENTS + (k + 1) * LC], h_leaf[:])
-            h_child = work.tile([H, LC], BF16, name="h_child")
-            nc.vector.tensor_copy(halves(h_child[:]), split(h_leaf[:]))
-            h_sum = work.tile([H, PC], BF16, name="h_sum")
-            nc.vector.tensor_tensor(h_sum[:], split(h_leaf[:])[:, 0, :], split(h_leaf[:])[:, 1, :], ADD)
-            c_leaves.append(c_leaf)
-            h_children.append(h_child)
-            h_sums.append(h_sum)
+            c_leaf.append(work.tile([H, LC], F32, name="c_leaf"))
+            nc.vector.tensor_tensor(c_leaf[k][:], i_leaf[:], u_leaf[:], MULT)
+            o_leaf.append(activate("o_leaf", LC, SIGMOID, z[GATE_O][:], GATE_O))
 
+        h_child, h_sum = [], []
+        for k in range(CHUNKS):
+            tanh_c_leaf = work.tile([H, LC], F32, name="tanh_c_leaf")
+            nc.scalar.activation(tanh_c_leaf[:], c_leaf[k][:], TANH)
+            h_leaf = work.tile([H, LC], F32, name="h_leaf")
+            nc.vector.tensor_tensor(h_leaf[:], o_leaf[k][:], tanh_c_leaf[:], MULT)
+            h_child.append(work.tile([H, LC], BF16, name="h_child"))
+            nc.vector.tensor_copy(halves(h_child[k][:]), split(h_leaf[:]))
+            h_sum.append(work.tile([H, PC], BF16, name="h_sum"))
+            nc.vector.tensor_tensor(h_sum[k][:], split(h_leaf[:])[:, 0, :], split(h_leaf[:])[:, 1, :], ADD)
+            nc.sync.dma_start(out[:, PARENTS + k * LC : PARENTS + (k + 1) * LC], h_leaf[:])
+
+        c_parent, o_parent = [], []
         for k in range(CHUNKS):
             z = z_parent[k]
-            nc.tensor.matmul(z[GATE_F][:], block(r_sb, GATE_F), h_children[k][:], start=False, stop=True)
+            nc.tensor.matmul(z[GATE_F][:], block(r_sb, GATE_F), h_child[k][:], start=False, stop=True)
             for gate in (GATE_I, GATE_U, GATE_O):
-                nc.tensor.matmul(z[gate][:], block(r_sb, gate), h_sums[k][:], start=False, stop=True)
+                nc.tensor.matmul(z[gate][:], block(r_sb, gate), h_sum[k][:], start=False, stop=True)
             f_child = activate("f_child", LC, SIGMOID, z[GATE_F][:], GATE_F)
             fc_child = work.tile([H, LC], F32, name="fc_child")
-            nc.vector.tensor_tensor(halves(fc_child[:]), halves(f_child[:]), split(c_leaves[k][:]), MULT)
-            i_parent = activate("i_parent", PC, SIGMOID, z[GATE_I][:], GATE_I)
-            u_parent = activate("u_parent", PC, TANH, z[GATE_U][:], GATE_U)
-            o_parent = activate("o_parent", PC, SIGMOID, z[GATE_O][:], GATE_O)
+            nc.vector.tensor_tensor(halves(fc_child[:]), halves(f_child[:]), split(c_leaf[k][:]), MULT)
             fc_sum = work.tile([H, PC], F32, name="fc_sum")
             nc.vector.tensor_tensor(fc_sum[:], fc_child[:, :PC], fc_child[:, PC:], ADD)
+            i_parent = activate("i_parent", PC, SIGMOID, z[GATE_I][:], GATE_I)
+            u_parent = activate("u_parent", PC, TANH, z[GATE_U][:], GATE_U)
             iu_parent = work.tile([H, PC], F32, name="iu_parent")
             nc.vector.tensor_tensor(iu_parent[:], i_parent[:], u_parent[:], MULT)
-            c_parent = work.tile([H, PC], F32, name="c_parent")
-            nc.vector.tensor_tensor(c_parent[:], iu_parent[:], fc_sum[:], ADD)
+            c_parent.append(work.tile([H, PC], F32, name="c_parent"))
+            nc.vector.tensor_tensor(c_parent[k][:], iu_parent[:], fc_sum[:], ADD)
+            o_parent.append(activate("o_parent", PC, SIGMOID, z[GATE_O][:], GATE_O))
+
+        for k in range(CHUNKS):
             tanh_c_parent = work.tile([H, PC], F32, name="tanh_c_parent")
-            nc.scalar.activation(tanh_c_parent[:], c_parent[:], TANH)
+            nc.scalar.activation(tanh_c_parent[:], c_parent[k][:], TANH)
             h_parent = work.tile([H, PC], F32, name="h_parent")
-            nc.vector.tensor_tensor(h_parent[:], o_parent[:], tanh_c_parent[:], MULT)
+            nc.vector.tensor_tensor(h_parent[:], o_parent[k][:], tanh_c_parent[:], MULT)
             nc.sync.dma_start(out[:, k * PC : (k + 1) * PC], h_parent[:])

@@ -96,10 +96,10 @@ def tile_treemodel_kernel(tc, table, w, r, b, offs, out):
         for k in range(CHUNKS):
             tanh_c_leaf = work.tile([H, LC], F32, name="tanh_c_leaf")
             nc.scalar.activation(tanh_c_leaf[:], c_leaf[k][:], TANH)
+            h_child.append(work.tile([H, LC], BF16, name="h_child"))
+            nc.vector.tensor_tensor(halves(h_child[k][:]), split(o_leaf[k][:]), split(tanh_c_leaf[:]), MULT)
             h_leaf = work.tile([H, LC], F32, name="h_leaf")
             nc.vector.tensor_tensor(h_leaf[:], o_leaf[k][:], tanh_c_leaf[:], MULT)
-            h_child.append(work.tile([H, LC], BF16, name="h_child"))
-            nc.vector.tensor_copy(halves(h_child[k][:]), split(h_leaf[:]))
             h_sum.append(work.tile([H, PC], BF16, name="h_sum"))
             nc.vector.tensor_tensor(h_sum[k][:], split(h_leaf[:])[:, 0, :], split(h_leaf[:])[:, 1, :], ADD)
             nc.sync.dma_start(out[:, PARENTS + k * LC : PARENTS + (k + 1) * LC], h_leaf[:])

@@ -14,6 +14,7 @@ GATE_I, GATE_O, GATE_U, GATE_F = 0, 1, 2, 3
 CHUNKS = 2
 PC = PARENTS // CHUNKS
 LC = 2 * PC
+LEAVES = 2 * PARENTS
 
 FLOPS = 2 * H * H * (3 * 2 * PARENTS + 4 * PARENTS + 3 * PARENTS + 2 * PARENTS)
 
@@ -58,7 +59,7 @@ def tile_treemodel_kernel(tc, table, w, r, b, offs, out):
         def halves(tile_ap):
             return tile_ap.rearrange("p (two j) -> p two j", two=2)
 
-        z_leaf, z_parent = [], []
+        z_leaf = []
         for k in range(CHUNKS):
             z = {}
             for gate in (GATE_I, GATE_U, GATE_O):
@@ -67,65 +68,76 @@ def tile_treemodel_kernel(tc, table, w, r, b, offs, out):
                     z[gate][:], block(w_sb, gate), looked_up(PARENTS + k * LC, LC), start=True, stop=True
                 )
             z_leaf.append(z)
-        for k in range(CHUNKS):
-            z = {}
-            for gate in (GATE_I, GATE_U, GATE_O):
-                z[gate] = psum.tile([H, PC], F32, name=f"z_parent{gate}", tag="bank")
-                nc.tensor.matmul(z[gate][:], block(w_sb, gate), looked_up(k * PC, PC), start=True, stop=False)
-            z[GATE_F] = psum.tile([H, LC], F32, name="z_forget", tag="bank")
-            for child in range(2):
-                nc.tensor.matmul(
-                    z[GATE_F][:, child * PC : (child + 1) * PC],
-                    block(w_sb, GATE_F),
-                    looked_up(k * PC, PC),
-                    start=(child == 0),
-                    stop=False,
-                )
-            z_parent.append(z)
+        z_forget = psum.tile([H, LEAVES], F32, name="z_forget", tag="bank")
+        for child in range(2):
+            nc.tensor.matmul(
+                z_forget[:, child * PARENTS : (child + 1) * PARENTS],
+                block(w_sb, GATE_F),
+                looked_up(0, PARENTS),
+                start=(child == 0),
+                stop=False,
+            )
+        z_parent = {}
+        for gate in (GATE_I, GATE_U, GATE_O):
+            z_parent[gate] = psum.tile([H, PARENTS], F32, name=f"z_parent{gate}", tag="bank")
+            nc.tensor.matmul(z_parent[gate][:], block(w_sb, gate), looked_up(0, PARENTS), start=True, stop=False)
 
-        c_leaf, o_leaf = [], []
+        c_leaf = held.tile([H, LEAVES], F32, name="c_leaf")
+        h_leaf = held.tile([H, LEAVES], F32, name="h_leaf")
+        h_child = held.tile([H, LEAVES], BF16, name="h_child")
+        h_sum = held.tile([H, PARENTS], BF16, name="h_sum")
         for k in range(CHUNKS):
+            leaves = slice(k * LC, (k + 1) * LC)
+            parents = slice(k * PC, (k + 1) * PC)
             z = z_leaf[k]
             i_leaf = activate("i_leaf", LC, SIGMOID, z[GATE_I][:], GATE_I)
             u_leaf = activate("u_leaf", LC, TANH, z[GATE_U][:], GATE_U)
-            c_leaf.append(work.tile([H, LC], F32, name="c_leaf"))
-            nc.vector.tensor_tensor(c_leaf[k][:], i_leaf[:], u_leaf[:], MULT)
-            o_leaf.append(activate("o_leaf", LC, SIGMOID, z[GATE_O][:], GATE_O))
-
-        h_child, h_sum = [], []
-        for k in range(CHUNKS):
+            nc.vector.tensor_tensor(c_leaf[:, leaves], i_leaf[:], u_leaf[:], MULT)
+            o_leaf = activate("o_leaf", LC, SIGMOID, z[GATE_O][:], GATE_O)
             tanh_c_leaf = work.tile([H, LC], F32, name="tanh_c_leaf")
-            nc.scalar.activation(tanh_c_leaf[:], c_leaf[k][:], TANH)
-            h_child.append(work.tile([H, LC], BF16, name="h_child"))
-            nc.vector.tensor_tensor(halves(h_child[k][:]), split(o_leaf[k][:]), split(tanh_c_leaf[:]), MULT)
-            h_leaf = work.tile([H, LC], F32, name="h_leaf")
-            nc.vector.tensor_tensor(h_leaf[:], o_leaf[k][:], tanh_c_leaf[:], MULT)
-            h_sum.append(work.tile([H, PC], BF16, name="h_sum"))
-            nc.vector.tensor_tensor(h_sum[k][:], split(h_leaf[:])[:, 0, :], split(h_leaf[:])[:, 1, :], ADD)
-            nc.sync.dma_start(out[:, PARENTS + k * LC : PARENTS + (k + 1) * LC], h_leaf[:])
+            nc.scalar.activation(tanh_c_leaf[:], c_leaf[:, leaves], TANH)
+            nc.vector.tensor_tensor(
+                halves(h_child[:])[:, :, parents], split(o_leaf[:]), split(tanh_c_leaf[:]), MULT
+            )
+            nc.vector.tensor_tensor(h_leaf[:, leaves], o_leaf[:], tanh_c_leaf[:], MULT)
+            pair = split(h_leaf[:, leaves])
+            nc.vector.tensor_tensor(h_sum[:, parents], pair[:, 0, :], pair[:, 1, :], ADD)
+        nc.sync.dma_start(out[:, PARENTS:], h_leaf[:])
 
-        c_parent, o_parent = [], []
+        nc.tensor.matmul(z_forget[:], block(r_sb, GATE_F), h_child[:], start=False, stop=True)
+        for gate in (GATE_I, GATE_U, GATE_O):
+            nc.tensor.matmul(z_parent[gate][:], block(r_sb, gate), h_sum[:], start=False, stop=True)
+
+        fc_sum = []
         for k in range(CHUNKS):
-            z = z_parent[k]
-            nc.tensor.matmul(z[GATE_F][:], block(r_sb, GATE_F), h_child[k][:], start=False, stop=True)
-            for gate in (GATE_I, GATE_U, GATE_O):
-                nc.tensor.matmul(z[gate][:], block(r_sb, gate), h_sum[k][:], start=False, stop=True)
-            f_child = activate("f_child", LC, SIGMOID, z[GATE_F][:], GATE_F)
+            parents = slice(k * PC, (k + 1) * PC)
+            f_child = work.tile([H, LC], F32, name="f_child")
+            nc.scalar.activation(
+                halves(f_child[:]),
+                halves(z_forget[:])[:, :, parents],
+                SIGMOID,
+                bias=bias[:, GATE_F : GATE_F + 1],
+            )
             fc_child = work.tile([H, LC], F32, name="fc_child")
-            nc.vector.tensor_tensor(halves(fc_child[:]), halves(f_child[:]), split(c_leaf[k][:]), MULT)
-            fc_sum = work.tile([H, PC], F32, name="fc_sum")
-            nc.vector.tensor_tensor(fc_sum[:], fc_child[:, :PC], fc_child[:, PC:], ADD)
-            i_parent = activate("i_parent", PC, SIGMOID, z[GATE_I][:], GATE_I)
-            u_parent = activate("u_parent", PC, TANH, z[GATE_U][:], GATE_U)
+            nc.vector.tensor_tensor(
+                halves(fc_child[:]), halves(f_child[:]), split(c_leaf[:, k * LC : (k + 1) * LC]), MULT
+            )
+            fc_sum.append(work.tile([H, PC], F32, name="fc_sum"))
+            nc.vector.tensor_tensor(fc_sum[k][:], fc_child[:, :PC], fc_child[:, PC:], ADD)
+        c_parent = []
+        for k in range(CHUNKS):
+            parents = slice(k * PC, (k + 1) * PC)
+            i_parent = activate("i_parent", PC, SIGMOID, z_parent[GATE_I][:, parents], GATE_I)
+            u_parent = activate("u_parent", PC, TANH, z_parent[GATE_U][:, parents], GATE_U)
             iu_parent = work.tile([H, PC], F32, name="iu_parent")
             nc.vector.tensor_tensor(iu_parent[:], i_parent[:], u_parent[:], MULT)
             c_parent.append(work.tile([H, PC], F32, name="c_parent"))
-            nc.vector.tensor_tensor(c_parent[k][:], iu_parent[:], fc_sum[:], ADD)
-            o_parent.append(activate("o_parent", PC, SIGMOID, z[GATE_O][:], GATE_O))
-
+            nc.vector.tensor_tensor(c_parent[k][:], iu_parent[:], fc_sum[k][:], ADD)
+        o_parent = activate("o_parent", PARENTS, SIGMOID, z_parent[GATE_O][:], GATE_O)
         for k in range(CHUNKS):
+            parents = slice(k * PC, (k + 1) * PC)
             tanh_c_parent = work.tile([H, PC], F32, name="tanh_c_parent")
             nc.scalar.activation(tanh_c_parent[:], c_parent[k][:], TANH)
             h_parent = work.tile([H, PC], F32, name="h_parent")
-            nc.vector.tensor_tensor(h_parent[:], o_parent[k][:], tanh_c_parent[:], MULT)
-            nc.sync.dma_start(out[:, k * PC : (k + 1) * PC], h_parent[:])
+            nc.vector.tensor_tensor(h_parent[:], o_parent[:, parents], tanh_c_parent[:], MULT)
+            nc.sync.dma_start(out[:, parents], h_parent[:])

@@ -59,85 +59,78 @@ def tile_treemodel_kernel(tc, table, w, r, b, offs, out):
         def halves(tile_ap):
             return tile_ap.rearrange("p (two j) -> p two j", two=2)
 
-        z_leaf = []
+        z_leaf = [{} for k in range(CHUNKS)]
+        for gates in ((GATE_I, GATE_U), (GATE_O,)):
+            for k in range(CHUNKS):
+                for gate in gates:
+                    z_leaf[k][gate] = psum.tile([H, LC], F32, name=f"z_leaf{gate}", tag="bank")
+                    nc.tensor.matmul(
+                        z_leaf[k][gate][:], block(w_sb, gate), looked_up(PARENTS + k * LC, LC), start=True, stop=True
+                    )
+        z_parent = [{} for k in range(CHUNKS)]
         for k in range(CHUNKS):
-            z = {}
-            for gate in (GATE_I, GATE_U, GATE_O):
-                z[gate] = psum.tile([H, LC], F32, name=f"z_leaf{gate}", tag="bank")
+            z_parent[k][GATE_F] = psum.tile([H, LC], F32, name="z_forget", tag="bank")
+            for child in range(2):
                 nc.tensor.matmul(
-                    z[gate][:], block(w_sb, gate), looked_up(PARENTS + k * LC, LC), start=True, stop=True
+                    z_parent[k][GATE_F][:, child * PC : (child + 1) * PC],
+                    block(w_sb, GATE_F),
+                    looked_up(k * PC, PC),
+                    start=(child == 0),
+                    stop=False,
                 )
-            z_leaf.append(z)
-        z_forget = psum.tile([H, LEAVES], F32, name="z_forget", tag="bank")
-        for child in range(2):
-            nc.tensor.matmul(
-                z_forget[:, child * PARENTS : (child + 1) * PARENTS],
-                block(w_sb, GATE_F),
-                looked_up(0, PARENTS),
-                start=(child == 0),
-                stop=False,
-            )
-        z_parent = {}
         for gate in (GATE_I, GATE_U, GATE_O):
-            z_parent[gate] = psum.tile([H, PARENTS], F32, name=f"z_parent{gate}", tag="bank")
-            nc.tensor.matmul(z_parent[gate][:], block(w_sb, gate), looked_up(0, PARENTS), start=True, stop=False)
+            for k in range(CHUNKS):
+                z_parent[k][gate] = psum.tile([H, PC], F32, name=f"z_parent{gate}", tag="bank")
+                nc.tensor.matmul(z_parent[k][gate][:], block(w_sb, gate), looked_up(k * PC, PC), start=True, stop=False)
 
-        c_leaf = held.tile([H, LEAVES], F32, name="c_leaf")
-        h_leaf = held.tile([H, LEAVES], F32, name="h_leaf")
-        h_child = held.tile([H, LEAVES], BF16, name="h_child")
-        h_sum = held.tile([H, PARENTS], BF16, name="h_sum")
+        c_leaf = []
         for k in range(CHUNKS):
-            leaves = slice(k * LC, (k + 1) * LC)
-            parents = slice(k * PC, (k + 1) * PC)
-            z = z_leaf[k]
-            i_leaf = activate("i_leaf", LC, SIGMOID, z[GATE_I][:], GATE_I)
-            u_leaf = activate("u_leaf", LC, TANH, z[GATE_U][:], GATE_U)
-            nc.vector.tensor_tensor(c_leaf[:, leaves], i_leaf[:], u_leaf[:], MULT)
-            o_leaf = activate("o_leaf", LC, SIGMOID, z[GATE_O][:], GATE_O)
+            i_leaf = activate("i_leaf", LC, SIGMOID, z_leaf[k][GATE_I][:], GATE_I)
+            u_leaf = activate("u_leaf", LC, TANH, z_leaf[k][GATE_U][:], GATE_U)
+            c_leaf.append(work.tile([H, LC], F32, name="c_leaf"))
+            nc.vector.tensor_tensor(c_leaf[k][:], i_leaf[:], u_leaf[:], MULT)
+        h_leaf = held.tile([H, LEAVES], F32, name="h_leaf")
+        h_child = []
+        for k in range(CHUNKS):
+            o_leaf = activate("o_leaf", LC, SIGMOID, z_leaf[k][GATE_O][:], GATE_O)
             tanh_c_leaf = work.tile([H, LC], F32, name="tanh_c_leaf")
-            nc.scalar.activation(tanh_c_leaf[:], c_leaf[:, leaves], TANH)
-            nc.vector.tensor_tensor(
-                halves(h_child[:])[:, :, parents], split(o_leaf[:]), split(tanh_c_leaf[:]), MULT
-            )
-            nc.vector.tensor_tensor(h_leaf[:, leaves], o_leaf[:], tanh_c_leaf[:], MULT)
-            pair = split(h_leaf[:, leaves])
-            nc.vector.tensor_tensor(h_sum[:, parents], pair[:, 0, :], pair[:, 1, :], ADD)
+            nc.scalar.activation(tanh_c_leaf[:], c_leaf[k][:], TANH)
+            h_child.append(work.tile([H, LC], BF16, name="h_child"))
+            nc.vector.tensor_tensor(halves(h_child[k][:]), split(o_leaf[:]), split(tanh_c_leaf[:]), MULT)
+            nc.vector.tensor_tensor(h_leaf[:, k * LC : (k + 1) * LC], o_leaf[:], tanh_c_leaf[:], MULT)
         nc.sync.dma_start(out[:, PARENTS:], h_leaf[:])
 
-        nc.tensor.matmul(z_forget[:], block(r_sb, GATE_F), h_child[:], start=False, stop=True)
+        for k in range(CHUNKS):
+            nc.tensor.matmul(z_parent[k][GATE_F][:], block(r_sb, GATE_F), h_child[k][:], start=False, stop=True)
         for gate in (GATE_I, GATE_U, GATE_O):
-            nc.tensor.matmul(z_parent[gate][:], block(r_sb, gate), h_sum[:], start=False, stop=True)
-
+            for k in range(CHUNKS):
+                for child in range(2):
+                    nc.tensor.matmul(
+                        z_parent[k][gate][:],
+                        block(r_sb, gate),
+                        h_child[k][:, child * PC : (child + 1) * PC],
+                        start=False,
+                        stop=(child == 1),
+                    )
         fc_sum = []
         for k in range(CHUNKS):
-            parents = slice(k * PC, (k + 1) * PC)
-            f_child = work.tile([H, LC], F32, name="f_child")
-            nc.scalar.activation(
-                halves(f_child[:]),
-                halves(z_forget[:])[:, :, parents],
-                SIGMOID,
-                bias=bias[:, GATE_F : GATE_F + 1],
-            )
+            f_child = activate("f_child", LC, SIGMOID, z_parent[k][GATE_F][:], GATE_F)
             fc_child = work.tile([H, LC], F32, name="fc_child")
-            nc.vector.tensor_tensor(
-                halves(fc_child[:]), halves(f_child[:]), split(c_leaf[:, k * LC : (k + 1) * LC]), MULT
-            )
+            nc.vector.tensor_tensor(halves(fc_child[:]), halves(f_child[:]), split(c_leaf[k][:]), MULT)
             fc_sum.append(work.tile([H, PC], F32, name="fc_sum"))
             nc.vector.tensor_tensor(fc_sum[k][:], fc_child[:, :PC], fc_child[:, PC:], ADD)
         c_parent = []
         for k in range(CHUNKS):
-            parents = slice(k * PC, (k + 1) * PC)
-            i_parent = activate("i_parent", PC, SIGMOID, z_parent[GATE_I][:, parents], GATE_I)
-            u_parent = activate("u_parent", PC, TANH, z_parent[GATE_U][:, parents], GATE_U)
+            i_parent = activate("i_parent", PC, SIGMOID, z_parent[k][GATE_I][:], GATE_I)
+            u_parent = activate("u_parent", PC, TANH, z_parent[k][GATE_U][:], GATE_U)
             iu_parent = work.tile([H, PC], F32, name="iu_parent")
             nc.vector.tensor_tensor(iu_parent[:], i_parent[:], u_parent[:], MULT)
             c_parent.append(work.tile([H, PC], F32, name="c_parent"))
             nc.vector.tensor_tensor(c_parent[k][:], iu_parent[:], fc_sum[k][:], ADD)
-        o_parent = activate("o_parent", PARENTS, SIGMOID, z_parent[GATE_O][:], GATE_O)
+        o_parent = [activate("o_parent", PC, SIGMOID, z_parent[k][GATE_O][:], GATE_O) for k in range(CHUNKS)]
         for k in range(CHUNKS):
-            parents = slice(k * PC, (k + 1) * PC)
             tanh_c_parent = work.tile([H, PC], F32, name="tanh_c_parent")
             nc.scalar.activation(tanh_c_parent[:], c_parent[k][:], TANH)
             h_parent = work.tile([H, PC], F32, name="h_parent")
-            nc.vector.tensor_tensor(h_parent[:], o_parent[:, parents], tanh_c_parent[:], MULT)
-            nc.sync.dma_start(out[:, parents], h_parent[:])
+            nc.vector.tensor_tensor(h_parent[:], o_parent[k][:], tanh_c_parent[:], MULT)
+            nc.sync.dma_start(out[:, k * PC : (k + 1) * PC], h_parent[:])

@@ -26,12 +26,12 @@ def tile_treemodel_kernel(tc, table, w, r, b, offs, out):
         tc.tile_pool(name="work", bufs=CHUNKS) as work,
         tc.psum_pool(name="psum", bufs=8) as psum,
     ):
-        offsets = held.tile([H, N // 16], U16, name="offsets")
-        nc.sync.dma_start(offsets[:], offs)
         table_sb = held.tile([H, V], BF16, name="table_sb")
         nc.scalar.dma_start(table_sb[:], table)
         w_sb = held.tile([H, 4 * H], BF16, name="w_sb")
         nc.sync.dma_start(w_sb[:], w)
+        offsets = held.tile([H, N // 16], U16, name="offsets")
+        nc.sync.dma_start(offsets[:], offs)
         bias = held.tile([H, 4], F32, name="bias")
         with nc.allow_non_contiguous_dma(reason="512 floats, one to a partition and gate"):
             nc.scalar.dma_start(bias[:], b.rearrange("(g n) one -> n (g one)", n=H))

@@ -29,14 +29,15 @@ def tile_treemodel_kernel(tc, table, w, r, b, offs, out):
         table_sb = held.tile([H, V], BF16, name="table_sb")
         nc.scalar.dma_start(table_sb[:], table)
         w_sb = held.tile([H, 4 * H], BF16, name="w_sb")
-        nc.sync.dma_start(w_sb[:], w)
+        nc.sync.dma_start(w_sb[:, :H], w[:, :H])
         offsets = held.tile([H, N // 16], U16, name="offsets")
         nc.sync.dma_start(offsets[:], offs)
         bias = held.tile([H, 4], F32, name="bias")
         with nc.allow_non_contiguous_dma(reason="512 floats, one to a partition and gate"):
-            nc.scalar.dma_start(bias[:], b.rearrange("(g n) one -> n (g one)", n=H))
+            nc.sync.dma_start(bias[:], b.rearrange("(g n) one -> n (g one)", n=H))
+        nc.scalar.dma_start(w_sb[:, H:], w[:, H:])
         r_sb = held.tile([H, 4 * H], BF16, name="r_sb")
-        nc.sync.dma_start(r_sb[:], r)
+        nc.gpsimd.dma_start(r_sb[:], r)
 
         warm = held.tile([H, 1], F32, name="warm")
         nc.vector.memset(warm[:], 0.0)

@@ -79,10 +79,12 @@ def tile_treemodel_kernel(tc, table, w, r, b, offs, out):
                     start=(child == 0),
                     stop=False,
                 )
-        for gate in (GATE_I, GATE_U, GATE_O):
+        for gate in (GATE_I, GATE_U):
             for k in range(CHUNKS):
                 z_parent[k][gate] = psum.tile([H, PC], F32, name=f"z_parent{gate}", tag="bank")
                 nc.tensor.matmul(z_parent[k][gate][:], block(w_sb, gate), looked_up(k * PC, PC), start=True, stop=False)
+        z_out = psum.tile([H, PARENTS], F32, name="z_out", tag="bank")
+        nc.tensor.matmul(z_out[:], block(w_sb, GATE_O), looked_up(0, PARENTS), start=True, stop=False)
 
         c_leaf = []
         for k in range(CHUNKS):
@@ -91,28 +93,37 @@ def tile_treemodel_kernel(tc, table, w, r, b, offs, out):
             c_leaf.append(work.tile([H, LC], F32, name="c_leaf"))
             nc.vector.tensor_tensor(c_leaf[k][:], i_leaf[:], u_leaf[:], MULT)
         h_leaf = held.tile([H, LEAVES], F32, name="h_leaf")
-        h_child = []
+        h_child = held.tile([H, CHUNKS, 2, PC], BF16, name="h_child")
         for k in range(CHUNKS):
             o_leaf = activate("o_leaf", LC, SIGMOID, z_leaf[k][GATE_O][:], GATE_O)
             tanh_c_leaf = work.tile([H, LC], F32, name="tanh_c_leaf")
             nc.scalar.activation(tanh_c_leaf[:], c_leaf[k][:], TANH)
-            h_child.append(work.tile([H, LC], BF16, name="h_child"))
-            nc.vector.tensor_tensor(halves(h_child[k][:]), split(o_leaf[:]), split(tanh_c_leaf[:]), MULT)
+            nc.vector.tensor_tensor(h_child[:, k], split(o_leaf[:]), split(tanh_c_leaf[:]), MULT)
             nc.vector.tensor_tensor(h_leaf[:, k * LC : (k + 1) * LC], o_leaf[:], tanh_c_leaf[:], MULT)
         nc.sync.dma_start(out[:, PARENTS:], h_leaf[:])
 
         for k in range(CHUNKS):
-            nc.tensor.matmul(z_parent[k][GATE_F][:], block(r_sb, GATE_F), h_child[k][:], start=False, stop=True)
-        for gate in (GATE_I, GATE_U, GATE_O):
+            nc.tensor.matmul(
+                halves(z_parent[k][GATE_F][:]), block(r_sb, GATE_F), h_child[:, k], start=False, stop=True
+            )
+        for gate in (GATE_I, GATE_U):
             for k in range(CHUNKS):
                 for child in range(2):
                     nc.tensor.matmul(
                         z_parent[k][gate][:],
                         block(r_sb, gate),
-                        h_child[k][:, child * PC : (child + 1) * PC],
+                        h_child[:, k, child, :],
                         start=False,
                         stop=(child == 1),
                     )
+        for child in range(2):
+            nc.tensor.matmul(
+                z_out[:].rearrange("p (k j) -> p k j", k=CHUNKS),
+                block(r_sb, GATE_O),
+                h_child[:, :, child, :],
+                start=False,
+                stop=(child == 1),
+            )
         fc_sum = []
         for k in range(CHUNKS):
             f_child = activate("f_child", LC, SIGMOID, z_parent[k][GATE_F][:], GATE_F)
@@ -128,10 +139,10 @@ def tile_treemodel_kernel(tc, table, w, r, b, offs, out):
             nc.vector.tensor_tensor(iu_parent[:], i_parent[:], u_parent[:], MULT)
             c_parent.append(work.tile([H, PC], F32, name="c_parent"))
             nc.vector.tensor_tensor(c_parent[k][:], iu_parent[:], fc_sum[k][:], ADD)
-        o_parent = [activate("o_parent", PC, SIGMOID, z_parent[k][GATE_O][:], GATE_O) for k in range(CHUNKS)]
+        o_parent = activate("o_parent", PARENTS, SIGMOID, z_out[:], GATE_O)
         for k in range(CHUNKS):
             tanh_c_parent = work.tile([H, PC], F32, name="tanh_c_parent")
             nc.scalar.activation(tanh_c_parent[:], c_parent[k][:], TANH)
             h_parent = work.tile([H, PC], F32, name="h_parent")
-            nc.vector.tensor_tensor(h_parent[:], o_parent[k][:], tanh_c_parent[:], MULT)
+            nc.vector.tensor_tensor(h_parent[:], o_parent[:, k * PC : (k + 1) * PC], tanh_c_parent[:], MULT)
             nc.sync.dma_start(out[:, k * PC : (k + 1) * PC], h_parent[:])

import concourse.mybir as mybir

BF16, F32, U16 = mybir.dt.bfloat16, mybir.dt.float32, mybir.dt.uint16
SIGMOID = mybir.ActivationFunctionType.Sigmoid
TANH = mybir.ActivationFunctionType.Tanh
MULT, ADD = mybir.AluOpType.mult, mybir.AluOpType.add

H = 128
V = 512
N = 768
PARENTS = 256
GATE_I, GATE_O, GATE_U, GATE_F = 0, 1, 2, 3

CHUNKS = 2
PC = PARENTS // CHUNKS
LC = 2 * PC
LEAVES = 2 * PARENTS

FLOPS = 2 * H * H * (3 * 2 * PARENTS + 4 * PARENTS + 3 * PARENTS + 2 * PARENTS)


def tile_treemodel_kernel(tc, table, w, r, b, offs, out):
    nc = tc.nc
    with (
        tc.tile_pool(name="held", bufs=1) as held,
        tc.tile_pool(name="work", bufs=CHUNKS) as work,
        tc.psum_pool(name="psum", bufs=8) as psum,
    ):
        table_sb = held.tile([H, V], BF16, name="table_sb")
        nc.scalar.dma_start(table_sb[:], table)
        w_sb = held.tile([H, 4 * H], BF16, name="w_sb")
        nc.sync.dma_start(w_sb[:, :H], w[:, :H])
        offsets = held.tile([H, N // 16], U16, name="offsets")
        nc.sync.dma_start(offsets[:], offs)
        bias = held.tile([H, 4], F32, name="bias")
        with nc.allow_non_contiguous_dma(reason="512 floats, one to a partition and gate"):
            nc.sync.dma_start(bias[:], b.rearrange("(g n) one -> n (g one)", n=H))
        nc.scalar.dma_start(w_sb[:, H:], w[:, H:])
        r_sb = held.tile([H, 4 * H], BF16, name="r_sb")
        nc.gpsimd.dma_start(r_sb[:], r)

        warm = held.tile([H, 1], F32, name="warm")
        nc.vector.memset(warm[:], 0.0)
        nc.scalar.activation(warm[:], warm[:], SIGMOID)

        def block(weights, gate):
            return weights[:, gate * H : (gate + 1) * H]

        def looked_up(first, count):
            return table_sb[:].indirect(offsets[:, first // 16 : (first + count) // 16])

        def activate(name, width, func, source, gate):
            result = work.tile([H, width], F32, name=name)
            nc.scalar.activation(result[:], source, func, bias=bias[:, gate : gate + 1])
            return result

        def split(tile_ap):
            return tile_ap.rearrange("p (j two) -> p two j", two=2)

        def halves(tile_ap):
            return tile_ap.rearrange("p (two j) -> p two j", two=2)

        z_leaf = [{} for k in range(CHUNKS)]
        for gates in ((GATE_I, GATE_U), (GATE_O,)):
            for k in range(CHUNKS):
                for gate in gates:
                    z_leaf[k][gate] = psum.tile([H, LC], F32, name=f"z_leaf{gate}", tag="bank")
                    nc.tensor.matmul(
                        z_leaf[k][gate][:], block(w_sb, gate), looked_up(PARENTS + k * LC, LC), start=True, stop=True
                    )
        z_parent = [{} for k in range(CHUNKS)]
        for k in range(CHUNKS):
            z_parent[k][GATE_F] = psum.tile([H, LC], F32, name="z_forget", tag="bank")
            for child in range(2):
                nc.tensor.matmul(
                    z_parent[k][GATE_F][:, child * PC : (child + 1) * PC],
                    block(w_sb, GATE_F),
                    looked_up(k * PC, PC),
                    start=(child == 0),
                    stop=False,
                )
        for gate in (GATE_I, GATE_U):
            for k in range(CHUNKS):
                z_parent[k][gate] = psum.tile([H, PC], F32, name=f"z_parent{gate}", tag="bank")
                nc.tensor.matmul(z_parent[k][gate][:], block(w_sb, gate), looked_up(k * PC, PC), start=True, stop=False)
        z_out = psum.tile([H, PARENTS], F32, name="z_out", tag="bank")
        nc.tensor.matmul(z_out[:], block(w_sb, GATE_O), looked_up(0, PARENTS), start=True, stop=False)

        c_leaf = []
        for k in range(CHUNKS):
            i_leaf = activate("i_leaf", LC, SIGMOID, z_leaf[k][GATE_I][:], GATE_I)
            u_leaf = activate("u_leaf", LC, TANH, z_leaf[k][GATE_U][:], GATE_U)
            c_leaf.append(work.tile([H, LC], F32, name="c_leaf"))
            nc.vector.tensor_tensor(c_leaf[k][:], i_leaf[:], u_leaf[:], MULT)
        h_leaf = held.tile([H, LEAVES], F32, name="h_leaf")
        h_child = held.tile([H, CHUNKS, 2, PC], BF16, name="h_child")
        for k in range(CHUNKS):
            o_leaf = activate("o_leaf", LC, SIGMOID, z_leaf[k][GATE_O][:], GATE_O)
            tanh_c_leaf = work.tile([H, LC], F32, name="tanh_c_leaf")
            nc.scalar.activation(tanh_c_leaf[:], c_leaf[k][:], TANH)
            nc.vector.tensor_tensor(h_child[:, k], split(o_leaf[:]), split(tanh_c_leaf[:]), MULT)
            nc.vector.tensor_tensor(h_leaf[:, k * LC : (k + 1) * LC], o_leaf[:], tanh_c_leaf[:], MULT)
        nc.sync.dma_start(out[:, PARENTS:], h_leaf[:])

        for k in range(CHUNKS):
            nc.tensor.matmul(
                halves(z_parent[k][GATE_F][:]), block(r_sb, GATE_F), h_child[:, k], start=False, stop=True
            )
        for gate in (GATE_I, GATE_U):
            for k in range(CHUNKS):
                for child in range(2):
                    nc.tensor.matmul(
                        z_parent[k][gate][:],
                        block(r_sb, gate),
                        h_child[:, k, child, :],
                        start=False,
                        stop=(child == 1),
                    )
        for child in range(2):
            nc.tensor.matmul(
                z_out[:].rearrange("p (k j) -> p k j", k=CHUNKS),
                block(r_sb, GATE_O),
                h_child[:, :, child, :],
                start=False,
                stop=(child == 1),
            )
        fc_sum = []
        for k in range(CHUNKS):
            f_child = activate("f_child", LC, SIGMOID, z_parent[k][GATE_F][:], GATE_F)
            fc_child = work.tile([H, LC], F32, name="fc_child")
            nc.vector.tensor_tensor(halves(fc_child[:]), halves(f_child[:]), split(c_leaf[k][:]), MULT)
            fc_sum.append(work.tile([H, PC], F32, name="fc_sum"))
            nc.vector.tensor_tensor(fc_sum[k][:], fc_child[:, :PC], fc_child[:, PC:], ADD)
        c_parent = []
        for k in range(CHUNKS):
            i_parent = activate("i_parent", PC, SIGMOID, z_parent[k][GATE_I][:], GATE_I)
            u_parent = activate("u_parent", PC, TANH, z_parent[k][GATE_U][:], GATE_U)
            iu_parent = work.tile([H, PC], F32, name="iu_parent")
            nc.vector.tensor_tensor(iu_parent[:], i_parent[:], u_parent[:], MULT)
            c_parent.append(work.tile([H, PC], F32, name="c_parent"))
            nc.vector.tensor_tensor(c_parent[k][:], iu_parent[:], fc_sum[k][:], ADD)
        o_parent = activate("o_parent", PARENTS, SIGMOID, z_out[:], GATE_O)
        for k in range(CHUNKS):
            tanh_c_parent = work.tile([H, PC], F32, name="tanh_c_parent")
            nc.scalar.activation(tanh_c_parent[:], c_parent[k][:], TANH)
            h_parent = work.tile([H, PC], F32, name="h_parent")
            nc.vector.tensor_tensor(h_parent[:], o_parent[:, k * PC : (k + 1) * PC], tanh_c_parent[:], MULT)
            nc.sync.dma_start(out[:, k * PC : (k + 1) * PC], h_parent[:])
